import numpy as np
import ml_dtypes


def mxq(x, axis, fmt="e4m3"):
    dtype, down = {"e4m3": (ml_dtypes.float8_e4m3fn, 7), "e5m2": (ml_dtypes.float8_e5m2, 14)}[fmt]
    v = np.moveaxis(np.asarray(x, np.float32).astype(ml_dtypes.bfloat16).astype(np.float64), axis, -1)
    blocks = v.reshape(v.shape[:-1] + (-1, 32))
    amax = np.abs(blocks).max(-1, keepdims=True)
    byte = np.maximum(np.where(amax > 0, np.frexp(amax)[1] - 1 + 127, 0) - down, 1)
    scale = np.exp2(byte - 127.0)
    codes = (blocks / scale).astype(np.float32).astype(dtype).astype(np.float64)
    return np.moveaxis((codes * scale).reshape(v.shape), -1, axis)


WIDE = False


def mx_kscale(k):
    if not WIDE:
        return np.ones(k)
    levels = np.array([10, -10, 5, -5, 0])
    if k % 512:
        return np.exp2(np.random.permutation(np.resize(levels, k // 32))).repeat(32)
    a = np.empty((k // 512, 16))
    for p in range(k // 512):
        a[p, :8] = np.random.permutation(np.resize(levels, 8))
        for g in range(8):
            far = levels[np.abs(levels - a[p, g]) >= 10]
            a[p, g + 8] = far[np.random.randint(len(far))]
    return np.exp2(a.ravel()).repeat(32)


BF16 = ml_dtypes.bfloat16


def bf(x):
    return np.asarray(x, np.float32).astype(BF16)


def f64(x):
    return np.asarray(x).astype(np.float64)


N, E, C = 6144, 3072, 1536
DENSITY = 0.01


def setup_inputs():
    s, t = mx_kscale(N), mx_kscale(C)
    member = np.random.uniform(size=(N, E)) < DENSITY
    return {"node_features": bf(np.random.standard_normal((N, C)) / s[:, None] * t[None, :]),
            "incidence": bf(member * s[:, None]),
            "W1": bf(np.random.standard_normal((C, C)) * np.sqrt(E) / np.sqrt(DENSITY * N * C) / t[:, None]),
            "b1": bf(np.random.standard_normal(C) * 0.1 * np.sqrt(E)),
            "edge_attention": bf(1.0 + np.random.standard_normal(E))}


def reference(node_features, incidence, W1, b1, edge_attention):
    agg = mxq(f64(incidence), 0, "e4m3").T @ mxq(f64(node_features), 0, "e4m3")
    lin = (mxq(agg, 1, "e4m3") @ mxq(f64(W1), 0, "e4m3")) + f64(b1)
    a = f64(edge_attention)
    e = np.exp(a - a.max())
    attn = e / e.sum()
    return lin * attn[:, None]

@@ -1,0 +1,288 @@
+from contextlib import ExitStack
+
+import concourse.mybir as mybir
+from concourse.masks import make_identity
+
+N_NODES, N_EDGES, N_CH = 6144, 3072, 1536
+FLOPS = 2 * N_EDGES * N_NODES * N_CH + 2 * N_EDGES * N_CH * N_CH
+
+F32 = mybir.dt.float32
+BF16 = mybir.dt.bfloat16
+U32 = mybir.dt.uint32
+U8 = mybir.dt.uint8
+FP8X4 = mybir.dt.float8_e4m3fn_x4
+ACT = mybir.ActivationFunctionType
+ALU = mybir.AluOpType
+AX = mybir.AxisListType
+
+P = 128
+PACK = 4
+K_PASS = P * PACK
+WIDE = 512
+NQ = N_NODES // K_PASS
+NG = N_CH // K_PASS
+NJ = N_EDGES // WIDE
+NT = WIDE // P
+N_TILES = N_EDGES // P
+
+RAW_BUFS = 4
+GRP_BUFS = 3
+V_COLS = 256
+HEAD_UNITS = (38, 17, 16)
+BLOCK_UNITS = {(2, 0): 7, (2, 1): 7, (2, 2): 7, (3, 0): 4, (3, 1): 4, (3, 2): 4, (4, 0): 4, (4, 1): 4, (4, 2): 5}
+BATCH = {(2, 1): 6, (2, 2): 6, (3, 0): 6, (3, 1): 6, (3, 2): 6, (4, 0): 6, (4, 1): 6, (4, 2): 6, (5, 0): 4, (5, 1): 4, (5, 2): 4}
+E1_HEAD = "svssvssv"
+E1_BODY = "svsv"
+
+
+def tile_heterogeneoustemporalhypergraphnn_pa_l_kernel(tc, node_features, incidence, W1, b1, edge_attention, out):
+    nc = tc.nc
+    with ExitStack() as ctx:
+        ctx.enter_context(tc.manual_schedule())
+        keep = ctx.enter_context(tc.tile_pool(name="keep", bufs=1))
+        stage = ctx.enter_context(tc.tile_pool(name="stage", bufs=2))
+        psum = ctx.enter_context(tc.psum_pool(name="psum", bufs=1))
+
+        state = {"bank": 7, "done": 0, "loaded": 0, "copied": 0}
+        raw, grp, codes, planes = {}, {}, {}, {}
+        pending = []
+
+        def new_bank(shape, dtype):
+            i = state["bank"]
+            state["bank"] = (i + 1) % 8
+            return psum.tile(shape, dtype, name="bank%d" % i, tag="bank%d" % i)
+
+        units = []
+        for q in range(NQ):
+            units.extend([("nf", q, 0), ("inc", 0, q), ("inc", 1, q)])
+        for g in (1, 2):
+            units.extend([("nf", q, g) for q in range(NQ)])
+        units.extend([("inc", 2, q) for q in range(NQ)])
+        units.extend([("w", g, n) for g in range(NG) for n in range(NG)])
+        for j in range(3, NJ):
+            units.extend([("inc", j, q) for q in range(NQ)])
+
+        def load(u):
+            kind, a, b = u
+            if kind == "nf":
+                src = node_features[a * K_PASS:(a + 1) * K_PASS, b * WIDE:(b + 1) * WIDE]
+            elif kind == "inc":
+                src = incidence[b * K_PASS:(b + 1) * K_PASS, a * WIDE:(a + 1) * WIDE]
+            else:
+                src = W1[a * K_PASS:(a + 1) * K_PASS, b * WIDE:(b + 1) * WIDE]
+            t = stage.tile([P, PACK, WIDE], BF16, name="raw", tag="raw", bufs=RAW_BUFS)
+            nc.sync.dma_start(out=t[:], in_=src.rearrange("(p j) w -> p j w", j=PACK))
+            raw[u] = t
+
+        def interleave(u):
+            t = raw.pop(u)
+            o = stage.tile([P, PACK * WIDE], BF16, name="grp", tag="grp", bufs=GRP_BUFS, align_bytes=64)
+            if u[0] == "nf":
+                src = t[:].rearrange("p j (m t) -> p t m j", t=PACK)
+                dst = o[:].rearrange("p (t m j) -> p t m j", t=PACK, j=PACK)
+                nc.vector.tensor_copy(out=dst[:, 0:2], in_=src[:, 0:2])
+                nc.scalar.copy(out=dst[:, 2:4], in_=src[:, 2:4])
+            else:
+                src = t[:].rearrange("p j w -> p w j")
+                dst = o[:].rearrange("p (w j) -> p w j", j=PACK)
+                nc.vector.tensor_copy(out=dst[:, 0:V_COLS], in_=src[:, 0:V_COLS])
+                nc.scalar.copy(out=dst[:, V_COLS:WIDE], in_=src[:, V_COLS:WIDE])
+            grp[u] = o
+
+        def quantize(u):
+            kind, a, b = u
+            o = grp.pop(u)
+            if kind == "nf":
+                c = keep.tile([P, WIDE], U32, name="nfc%d_%d" % (a, b), tag="nfc%d_%d" % (a, b), align_bytes=64)
+                s = keep.tile([P, P], U8, name="nfs%d_%d" % (a, b), tag="nfs%d_%d" % (a, b), align_bytes=64)
+                for t in range(NT):
+                    nc.vector.quantize_mx(out=c[:, t * P:(t + 1) * P].bitcast(FP8X4), scales=s[PACK * t:P, :],
+                                          in_=o[:, t * WIDE:(t + 1) * WIDE])
+            else:
+                if kind == "inc":
+                    c = keep.tile([P, WIDE], U32, name="ic%d" % b, tag="ic%d" % b, bufs=2, align_bytes=64)
+                    s = keep.tile([P, WIDE], U8, name="is%d" % b, tag="is%d" % b, bufs=2, align_bytes=64)
+                elif kind == "w":
+                    c = keep.tile([P, WIDE], U32, name="wc%d_%d" % (a, b), tag="wc%d_%d" % (a, b), align_bytes=64)
+                    s = keep.tile([P, WIDE], U8, name="ws%d_%d" % (a, b), tag="ws%d_%d" % (a, b), align_bytes=64)
+                else:
+                    c = keep.tile([P, WIDE], U32, name="ac%d" % b, tag="ac%d" % b, bufs=3, align_bytes=64)
+                    s = keep.tile([P, WIDE], U8, name="as%d" % b, tag="as%d" % b, bufs=3, align_bytes=64)
+                nc.vector.quantize_mx(out=c[:].bitcast(FP8X4), scales=s[:], in_=o[:])
+            codes[u] = c
+            planes[u] = s
+
+        def pump():
+            k = state["done"]
+            while state["copied"] < min(k + 2, len(units)):
+                interleave(units[state["copied"]])
+                state["copied"] += 1
+            while state["loaded"] < min(state["copied"] + RAW_BUFS, len(units)):
+                load(units[state["loaded"]])
+                state["loaded"] += 1
+            quantize(units[k])
+            state["done"] = k + 1
+
+        def advance(target):
+            while state["done"] < min(target, len(units)):
+                pump()
+
+        def pop(n):
+            for i in range(min(n, len(pending))):
+                pending.pop(0)()
+
+        ident_b = keep.tile([P, P], BF16, name="ident_b", tag="ident_b")
+        ident_f = keep.tile([P, P], F32, name="ident_f", tag="ident_f")
+        a_rows = keep.tile([P, P], BF16, name="a_rows", tag="a_rows")
+        warm = keep.tile([P, 1], F32, name="warm", tag="warm")
+        nc.gpsimd.memset(a_rows[:], 0.0)
+        nc.gpsimd.memset(warm[:], 0.0)
+        nc.sync.dma_start(out=a_rows[0:N_TILES, :], in_=edge_attention.rearrange("(c p) -> c p", p=P))
+        make_identity(nc, ident_b[:])
+        make_identity(nc, ident_f[:])
+        nc.scalar.activation(out=warm[:], in_=warm[:], func=ACT.Exp)
+        for i in range(RAW_BUFS):
+            load(units[i])
+        state["loaded"] = RAW_BUFS
+
+        a_col = keep.tile([P, N_TILES], F32, name="a_col", tag="a_col")
+        e_col = keep.tile([P, N_TILES], F32, name="e_col", tag="e_col")
+        attn = keep.tile([P, N_TILES], F32, name="attn", tag="attn")
+        stat = {}
+        for nm in ("pmax", "gmax", "nmax", "psumx", "gsum", "rsum"):
+            stat[nm] = keep.tile([P, 1], F32, name=nm, tag=nm)
+        a_t = new_bank([P, P], BF16)
+        nc.tensor.transpose(out=a_t[:], in_=a_rows[:], identity=ident_b[:])
+        nc.vector.tensor_copy(out=a_col[:], in_=a_t[:, 0:N_TILES])
+        nc.vector.reduce_max(out=stat["pmax"][:], in_=a_col[:], axis=AX.X)
+        state["bank"] = 7
+        m_t = new_bank([P, P], F32)
+        nc.tensor.matmul(out=m_t[:], lhsT=stat["pmax"][:].to_broadcast([P, P]), rhs=ident_f[:], start=True, stop=True)
+        nc.vector.reduce_max(out=stat["gmax"][:], in_=m_t[:], axis=AX.X)
+        nc.vector.tensor_scalar_mul(out=stat["nmax"][:], in0=stat["gmax"][:], scalar1=-1.0)
+        nc.scalar.activation(out=e_col[:], in_=a_col[:], func=ACT.Exp, bias=stat["nmax"][:], scale=1.0, accum_out=stat["psumx"][:])
+        state["bank"] = 7
+        s_t = new_bank([P, P], F32)
+        nc.tensor.matmul(out=s_t[:], lhsT=stat["psumx"][:].to_broadcast([P, P]), rhs=ident_f[:], start=True, stop=True)
+        interleave(units[0])
+        state["copied"] = 1
+        nc.vector.reduce_sum(out=stat["gsum"][:], in_=s_t[:], axis=AX.X)
+        nc.vector.reciprocal(out=stat["rsum"][:], in_=stat["gsum"][:])
+        nc.vector.tensor_scalar_mul(out=attn[:], in0=e_col[:], scalar1=stat["rsum"][:])
+        b1_all = keep.tile([P, N_CH], BF16, name="b1_all", tag="b1_all")
+
+        def s1_step(chunks, g, q, banks):
+            for j in chunks:
+                for t in range(NT):
+                    nc.tensor.matmul_mx(out=banks[(j, t)][:],
+                                        lhsT=codes[("nf", q, g)][:, t * P:(t + 1) * P].bitcast(FP8X4),
+                                        lhsT_scale=planes[("nf", q, g)][PACK * t:P, :],
+                                        rhs=codes[("inc", j, q)][:].bitcast(FP8X4),
+                                        rhs_scale=planes[("inc", j, q)][:],
+                                        start=(q == 0), stop=(q == NQ - 1))
+
+        def empty_s1(chunks, g, banks, who, split):
+            i = 0
+            for j in chunks:
+                ab = stage.tile([P, PACK, WIDE], BF16, name="aggb", tag="aggb", bufs=2)
+                for t in range(NT):
+                    if who[i] == "s":
+                        nc.scalar.copy(out=ab[:, t, :], in_=banks[(j, t)][:])
+                    else:
+                        nc.vector.tensor_copy(out=ab[:, t, :], in_=banks[(j, t)][:])
+                    i += 1
+                raw[("agg", j, g)] = ab
+            for j in chunks:
+                pending.append(lambda j=j: agg_interleave(("agg", j, g), split))
+                pending.append(lambda j=j: quantize(("agg", j, g)))
+
+        def agg_interleave(u, split):
+            ab = raw.pop(u)
+            o = stage.tile([P, PACK * WIDE], BF16, name="grp", tag="grp", bufs=GRP_BUFS, align_bytes=64)
+            src = ab[:].rearrange("p t e -> p e t")
+            dst = o[:].rearrange("p (e t) -> p e t", t=PACK)
+            if split:
+                nc.vector.tensor_copy(out=dst[:, 0:V_COLS], in_=src[:, 0:V_COLS])
+                nc.scalar.copy(out=dst[:, V_COLS:WIDE], in_=src[:, V_COLS:WIDE])
+            else:
+                nc.vector.tensor_copy(out=dst, in_=src)
+            grp[u] = o
+
+        groups = [(j, m, n) for j in range(NJ) for m in range(NT) for n in range(NG)]
+        bias_tiles = {}
+        s2_banks = {}
+        nxt = {"mm": 0}
+
+        def bias_tile(k):
+            j, m, n = groups[k]
+            e_tile = j * NT + m
+            ba = stage.tile([P, WIDE], F32, name="ba", tag="ba", bufs=2)
+            nc.scalar.activation(out=ba[:], in_=b1_all[:, n * WIDE:(n + 1) * WIDE], func=ACT.Copy, scale=attn[:, e_tile:e_tile + 1])
+            bias_tiles[k] = ba
+
+        def s2_group(k):
+            j, m, n = groups[k]
+            bank = new_bank([P, WIDE], F32)
+            for g in range(NG):
+                nc.tensor.matmul_mx(out=bank[:],
+                                    lhsT=codes[("agg", j, g)][:, m * P:(m + 1) * P].bitcast(FP8X4),
+                                    lhsT_scale=planes[("agg", j, g)][:, m * P:(m + 1) * P],
+                                    rhs=codes[("w", g, n)][:].bitcast(FP8X4),
+                                    rhs_scale=planes[("w", g, n)][:],
+                                    start=(g == 0), stop=(g == NG - 1))
+            s2_banks[k] = bank
+            pending.append(lambda: finish(k))
+
+        def finish(k):
+            j, m, n = groups[k]
+            e_tile = j * NT + m
+            ot = stage.tile([P, WIDE], F32, name="ot", tag="ot", bufs=4)
+            nc.vector.scalar_tensor_tensor(out=ot[:], in0=s2_banks.pop(k)[:], scalar=attn[:, e_tile:e_tile + 1],
+                                           in1=bias_tiles.pop(k)[:], op0=ALU.mult, op1=ALU.add)
+            nc.sync.dma_start(out=out[e_tile * P:(e_tile + 1) * P, n * WIDE:(n + 1) * WIDE], in_=ot[:])
+            if k + 1 < len(groups):
+                bias_tile(k + 1)
+
+        def batch(n):
+            for i in range(n):
+                s2_group(nxt["mm"])
+                nxt["mm"] += 1
+                pop(1)
+
+        base = 0
+        for g in range(NG):
+            banks = {}
+            for j in (0, 1):
+                for t in range(NT):
+                    banks[(j, t)] = new_bank([P, WIDE], F32)
+            for q in range(NQ):
+                advance(base + (HEAD_UNITS[g] * (q + 1) + NQ - 1) // NQ)
+                pop(1)
+                s1_step((0, 1), g, q, banks)
+                if g == 1 and q == 0:
+                    nc.sync.dma_start(out=b1_all[:], in_=b1.partition_broadcast(P))
+            base += HEAD_UNITS[g]
+            empty_s1((0, 1), g, banks, E1_HEAD, False)
+
+        for j in range(2, NJ):
+            for g in range(NG):
+                banks = {}
+                for t in range(NT):
+                    banks[(j, t)] = new_bank([P, WIDE], F32)
+                n_units = BLOCK_UNITS.get((j, g), 0)
+                for q in range(NQ):
+                    advance(base + (n_units * (q + 1) + NQ - 1) // NQ)
+                    pop(1)
+                    s1_step((j,), g, q, banks)
+                base += n_units
+                last = (j == NJ - 1 and g == NG - 1)
+                empty_s1((j,), g, banks, E1_BODY, last)
+                if (j, g) == (2, 1):
+                    bias_tile(0)
+                batch(BATCH.get((j, g), 0))
+        pop(len(pending))
+        while nxt["mm"] < len(groups):
+            s2_group(nxt["mm"])
+            nxt["mm"] += 1
+            pop(1)
+        pop(len(pending))

@@ -25,12 +25,15 @@ NJ = N_EDGES // WIDE
 NT = WIDE // P
 N_TILES = N_EDGES // P
 
-RAW_BUFS = 4
+RAW_BUFS = 7
 GRP_BUFS = 3
 V_COLS = 256
 HEAD_UNITS = (38, 17, 16)
 BLOCK_UNITS = {(2, 0): 7, (2, 1): 7, (2, 2): 7, (3, 0): 4, (3, 1): 4, (3, 2): 4, (4, 0): 4, (4, 1): 4, (4, 2): 5}
 BATCH = {(2, 1): 6, (2, 2): 6, (3, 0): 6, (3, 1): 6, (3, 2): 6, (4, 0): 6, (4, 1): 6, (4, 2): 6, (5, 0): 4, (5, 1): 4, (5, 2): 4}
+TAIL_GROUPS = 60
+BA_AHEAD = 2
+BA_AHEAD_TAIL = 5
 E1_HEAD = "svssvssv"
 E1_BODY = "svsv"
 
@@ -43,9 +46,24 @@ def tile_heterogeneoustemporalhypergraphnn_pa_l_kernel(tc, node_features, incide
         stage = ctx.enter_context(tc.tile_pool(name="stage", bufs=2))
         psum = ctx.enter_context(tc.psum_pool(name="psum", bufs=1))
 
-        state = {"bank": 7, "done": 0, "loaded": 0, "copied": 0}
-        raw, grp, codes, planes = {}, {}, {}, {}
+        state = {"bank": 7, "done": 0, "loaded": 0, "copied": 0, "spare": 0}
+        raw, grp, codes, planes, nf_planes = {}, {}, {}, {}, {}
         pending = []
+        ring = []
+
+        def raw_tile(u, shape, dtype):
+            assert len(ring) < RAW_BUFS or ring[len(ring) - RAW_BUFS][0], "the oldest slot is still in use"
+            ring.append([False])
+            raw[u] = (stage.tile(shape, dtype, name="raw", tag="raw", bufs=RAW_BUFS), ring[len(ring) - 1])
+            return raw[u][0]
+
+        def raw_done(u):
+            t, flag = raw.pop(u)
+            flag[0] = True
+            return t
+
+        def slots_free(n):
+            return all([len(ring) + i < RAW_BUFS or ring[len(ring) + i - RAW_BUFS][0] for i in range(n)])
 
         def new_bank(shape, dtype):
             i = state["bank"]
@@ -70,12 +88,11 @@ def tile_heterogeneoustemporalhypergraphnn_pa_l_kernel(tc, node_features, incide
                 src = incidence[b * K_PASS:(b + 1) * K_PASS, a * WIDE:(a + 1) * WIDE]
             else:
                 src = W1[a * K_PASS:(a + 1) * K_PASS, b * WIDE:(b + 1) * WIDE]
-            t = stage.tile([P, PACK, WIDE], BF16, name="raw", tag="raw", bufs=RAW_BUFS)
+            t = raw_tile(u, [P, PACK, WIDE], BF16)
             nc.sync.dma_start(out=t[:], in_=src.rearrange("(p j) w -> p j w", j=PACK))
-            raw[u] = t
 
         def interleave(u):
-            t = raw.pop(u)
+            t = raw_done(u)
             o = stage.tile([P, PACK * WIDE], BF16, name="grp", tag="grp", bufs=GRP_BUFS, align_bytes=64)
             if u[0] == "nf":
                 src = t[:].rearrange("p j (m t) -> p t m j", t=PACK)
@@ -94,10 +111,10 @@ def tile_heterogeneoustemporalhypergraphnn_pa_l_kernel(tc, node_features, incide
             o = grp.pop(u)
             if kind == "nf":
                 c = keep.tile([P, WIDE], U32, name="nfc%d_%d" % (a, b), tag="nfc%d_%d" % (a, b), align_bytes=64)
-                s = keep.tile([P, P], U8, name="nfs%d_%d" % (a, b), tag="nfs%d_%d" % (a, b), align_bytes=64)
-                for t in range(NT):
-                    nc.vector.quantize_mx(out=c[:, t * P:(t + 1) * P].bitcast(FP8X4), scales=s[PACK * t:P, :],
-                                          in_=o[:, t * WIDE:(t + 1) * WIDE])
+                if b == 0:
+                    nf_planes[a] = keep.tile([P, WIDE], U8, name="nfs%d" % a, tag="nfs%d" % a, align_bytes=64)
+                s = nf_planes[a][PACK * b:P, :]
+                nc.vector.quantize_mx(out=c[:].bitcast(FP8X4), scales=s, in_=o[:])
             else:
                 if kind == "inc":
                     c = keep.tile([P, WIDE], U32, name="ic%d" % b, tag="ic%d" % b, bufs=2, align_bytes=64)
@@ -117,7 +134,7 @@ def tile_heterogeneoustemporalhypergraphnn_pa_l_kernel(tc, node_features, incide
             while state["copied"] < min(k + 2, len(units)):
                 interleave(units[state["copied"]])
                 state["copied"] += 1
-            while state["loaded"] < min(state["copied"] + RAW_BUFS, len(units)):
+            while state["loaded"] < len(units) and slots_free(1 + state["spare"]):
                 load(units[state["loaded"]])
                 state["loaded"] += 1
             quantize(units[k])
@@ -137,7 +154,7 @@ def tile_heterogeneoustemporalhypergraphnn_pa_l_kernel(tc, node_features, incide
         warm = keep.tile([P, 1], F32, name="warm", tag="warm")
         nc.gpsimd.memset(a_rows[:], 0.0)
         nc.gpsimd.memset(warm[:], 0.0)
-        nc.sync.dma_start(out=a_rows[0:N_TILES, :], in_=edge_attention.rearrange("(c p) -> c p", p=P))
+        nc.scalar.dma_start(out=a_rows[0:N_TILES, :], in_=edge_attention.rearrange("(c p) -> c p", p=P))
         make_identity(nc, ident_b[:])
         make_identity(nc, ident_f[:])
         nc.scalar.activation(out=warm[:], in_=warm[:], func=ACT.Exp)
@@ -176,7 +193,7 @@ def tile_heterogeneoustemporalhypergraphnn_pa_l_kernel(tc, node_features, incide
                 for t in range(NT):
                     nc.tensor.matmul_mx(out=banks[(j, t)][:],
                                         lhsT=codes[("nf", q, g)][:, t * P:(t + 1) * P].bitcast(FP8X4),
-                                        lhsT_scale=planes[("nf", q, g)][PACK * t:P, :],
+                                        lhsT_scale=planes[("nf", q, g)][:, t * P:(t + 1) * P],
                                         rhs=codes[("inc", j, q)][:].bitcast(FP8X4),
                                         rhs_scale=planes[("inc", j, q)][:],
                                         start=(q == 0), stop=(q == NQ - 1))
@@ -184,20 +201,19 @@ def tile_heterogeneoustemporalhypergraphnn_pa_l_kernel(tc, node_features, incide
         def empty_s1(chunks, g, banks, who, split):
             i = 0
             for j in chunks:
-                ab = stage.tile([P, PACK, WIDE], BF16, name="aggb", tag="aggb", bufs=2)
+                ab = raw_tile(("agg", j, g), [P, PACK, WIDE], BF16)
                 for t in range(NT):
                     if who[i] == "s":
                         nc.scalar.copy(out=ab[:, t, :], in_=banks[(j, t)][:])
                     else:
                         nc.vector.tensor_copy(out=ab[:, t, :], in_=banks[(j, t)][:])
                     i += 1
-                raw[("agg", j, g)] = ab
             for j in chunks:
                 pending.append(lambda j=j: agg_interleave(("agg", j, g), split))
                 pending.append(lambda j=j: quantize(("agg", j, g)))
 
         def agg_interleave(u, split):
-            ab = raw.pop(u)
+            ab = raw_done(u)
             o = stage.tile([P, PACK * WIDE], BF16, name="grp", tag="grp", bufs=GRP_BUFS, align_bytes=64)
             src = ab[:].rearrange("p t e -> p e t")
             dst = o[:].rearrange("p (e t) -> p e t", t=PACK)
@@ -211,12 +227,15 @@ def tile_heterogeneoustemporalhypergraphnn_pa_l_kernel(tc, node_features, incide
         groups = [(j, m, n) for j in range(NJ) for m in range(NT) for n in range(NG)]
         bias_tiles = {}
         s2_banks = {}
-        nxt = {"mm": 0}
+        nxt = {"mm": 0, "ba": 0}
 
         def bias_tile(k):
             j, m, n = groups[k]
             e_tile = j * NT + m
-            ba = stage.tile([P, WIDE], F32, name="ba", tag="ba", bufs=2)
+            if k >= TAIL_GROUPS and k % 3 != 0:
+                ba = raw_tile(("ot", k), [P, WIDE], F32)
+            else:
+                ba = stage.tile([P, WIDE], F32, name="ot", tag="ot", bufs=4)
             nc.scalar.activation(out=ba[:], in_=b1_all[:, n * WIDE:(n + 1) * WIDE], func=ACT.Copy, scale=attn[:, e_tile:e_tile + 1])
             bias_tiles[k] = ba
 
@@ -236,12 +255,15 @@ def tile_heterogeneoustemporalhypergraphnn_pa_l_kernel(tc, node_features, incide
         def finish(k):
             j, m, n = groups[k]
             e_tile = j * NT + m
-            ot = stage.tile([P, WIDE], F32, name="ot", tag="ot", bufs=4)
+            ot = bias_tiles.pop(k)
             nc.vector.scalar_tensor_tensor(out=ot[:], in0=s2_banks.pop(k)[:], scalar=attn[:, e_tile:e_tile + 1],
-                                           in1=bias_tiles.pop(k)[:], op0=ALU.mult, op1=ALU.add)
+                                           in1=ot[:], op0=ALU.mult, op1=ALU.add)
             nc.sync.dma_start(out=out[e_tile * P:(e_tile + 1) * P, n * WIDE:(n + 1) * WIDE], in_=ot[:])
-            if k + 1 < len(groups):
-                bias_tile(k + 1)
+            if ("ot", k) in raw:
+                raw_done(("ot", k))
+            while nxt["ba"] < min(k + 1 + (BA_AHEAD_TAIL if k + 1 >= TAIL_GROUPS else BA_AHEAD), len(groups)):
+                bias_tile(nxt["ba"])
+                nxt["ba"] += 1
 
         def batch(n):
             for i in range(n):
@@ -256,6 +278,8 @@ def tile_heterogeneoustemporalhypergraphnn_pa_l_kernel(tc, node_features, incide
                 for t in range(NT):
                     banks[(j, t)] = new_bank([P, WIDE], F32)
             for q in range(NQ):
+                if q == NQ - 3:
+                    state["spare"] = 2
                 advance(base + (HEAD_UNITS[g] * (q + 1) + NQ - 1) // NQ)
                 pop(1)
                 s1_step((0, 1), g, q, banks)
@@ -270,6 +294,7 @@ def tile_heterogeneoustemporalhypergraphnn_pa_l_kernel(tc, node_features, incide
                 for t in range(NT):
                     banks[(j, t)] = new_bank([P, WIDE], F32)
                 n_units = BLOCK_UNITS.get((j, g), 0)
+                state["spare"] = 1
                 for q in range(NQ):
                     advance(base + (n_units * (q + 1) + NQ - 1) // NQ)
                     pop(1)
@@ -278,7 +303,9 @@ def tile_heterogeneoustemporalhypergraphnn_pa_l_kernel(tc, node_features, incide
                 last = (j == NJ - 1 and g == NG - 1)
                 empty_s1((j,), g, banks, E1_BODY, last)
                 if (j, g) == (2, 1):
-                    bias_tile(0)
+                    for i in range(BA_AHEAD):
+                        bias_tile(i)
+                    nxt["ba"] = BA_AHEAD
                 batch(BATCH.get((j, g), 0))
         pop(len(pending))
         while nxt["mm"] < len(groups):

@@ -95,15 +95,15 @@ def tile_heterogeneoustemporalhypergraphnn_pa_l_kernel(tc, node_features, incide
             t = raw_done(u)
             o = stage.tile([P, PACK * WIDE], BF16, name="grp", tag="grp", bufs=GRP_BUFS, align_bytes=64)
             if u[0] == "nf":
-                src = t[:].rearrange("p j (m t) -> p t m j", t=PACK)
-                dst = o[:].rearrange("p (t m j) -> p t m j", t=PACK, j=PACK)
-                nc.vector.tensor_copy(out=dst[:, 0:2], in_=src[:, 0:2])
-                nc.scalar.copy(out=dst[:, 2:4], in_=src[:, 2:4])
+                src = t[:].rearrange("p j (m t) -> p m j t", t=PACK)
+                dst = o[:].rearrange("p (t m j) -> p m j t", t=PACK, j=PACK)
+                nc.vector.tensor_copy(out=dst[:, 0:V_COLS // PACK], in_=src[:, 0:V_COLS // PACK])
+                nc.scalar.copy(out=dst[:, V_COLS // PACK:P], in_=src[:, V_COLS // PACK:P])
             else:
-                src = t[:].rearrange("p j w -> p w j")
-                dst = o[:].rearrange("p (w j) -> p w j", j=PACK)
-                nc.vector.tensor_copy(out=dst[:, 0:V_COLS], in_=src[:, 0:V_COLS])
-                nc.scalar.copy(out=dst[:, V_COLS:WIDE], in_=src[:, V_COLS:WIDE])
+                src = t[:].rearrange("p j (c i) -> p c j i", i=PACK)
+                dst = o[:].rearrange("p (c i j) -> p c j i", i=PACK, j=PACK)
+                nc.vector.tensor_copy(out=dst[:, 0:V_COLS // PACK], in_=src[:, 0:V_COLS // PACK])
+                nc.scalar.copy(out=dst[:, V_COLS // PACK:P], in_=src[:, V_COLS // PACK:P])
             grp[u] = o
 
         def quantize(u):
@@ -152,9 +152,13 @@ def tile_heterogeneoustemporalhypergraphnn_pa_l_kernel(tc, node_features, incide
         ident_f = keep.tile([P, P], F32, name="ident_f", tag="ident_f")
         a_rows = keep.tile([P, P], BF16, name="a_rows", tag="a_rows")
         warm = keep.tile([P, 1], F32, name="warm", tag="warm")
-        nc.gpsimd.memset(a_rows[:], 0.0)
+        ea_rows = edge_attention.rearrange("(c p) -> c p", p=P)
+        nc.scalar.dma_start(out=a_rows[0:16, :], in_=ea_rows[0:16, :])
+        nc.scalar.dma_start(out=a_rows[16:24, :], in_=ea_rows[16:24, :])
+        nc.scalar.dma_start(out=a_rows[24:32, :], in_=ea_rows[16:24, :])
+        nc.gpsimd.memset(a_rows[32:64, :], 0.0)
+        nc.gpsimd.memset(a_rows[64:128, :], 0.0)
         nc.gpsimd.memset(warm[:], 0.0)
-        nc.scalar.dma_start(out=a_rows[0:N_TILES, :], in_=edge_attention.rearrange("(c p) -> c p", p=P))
         make_identity(nc, ident_b[:])
         make_identity(nc, ident_f[:])
         nc.scalar.activation(out=warm[:], in_=warm[:], func=ACT.Exp)
@@ -215,11 +219,11 @@ def tile_heterogeneoustemporalhypergraphnn_pa_l_kernel(tc, node_features, incide
         def agg_interleave(u, split):
             ab = raw_done(u)
             o = stage.tile([P, PACK * WIDE], BF16, name="grp", tag="grp", bufs=GRP_BUFS, align_bytes=64)
-            src = ab[:].rearrange("p t e -> p e t")
-            dst = o[:].rearrange("p (e t) -> p e t", t=PACK)
+            src = ab[:].rearrange("p t (c i) -> p c t i", i=PACK)
+            dst = o[:].rearrange("p (c i t) -> p c t i", i=PACK, t=PACK)
             if split:
-                nc.vector.tensor_copy(out=dst[:, 0:V_COLS], in_=src[:, 0:V_COLS])
-                nc.scalar.copy(out=dst[:, V_COLS:WIDE], in_=src[:, V_COLS:WIDE])
+                nc.vector.tensor_copy(out=dst[:, 0:V_COLS // PACK], in_=src[:, 0:V_COLS // PACK])
+                nc.scalar.copy(out=dst[:, V_COLS // PACK:P], in_=src[:, V_COLS // PACK:P])
             else:
                 nc.vector.tensor_copy(out=dst, in_=src)
             grp[u] = o

@@ -26,6 +26,7 @@ NT = WIDE // P
 N_TILES = N_EDGES // P
 
 RAW_BUFS = 7
+PAIR_BUFS = 4
 GRP_BUFS = 3
 V_COLS = 256
 HEAD_UNITS = (38, 17, 16)
@@ -47,20 +48,28 @@ def tile_heterogeneoustemporalhypergraphnn_pa_l_kernel(tc, node_features, incide
         psum = ctx.enter_context(tc.psum_pool(name="psum", bufs=1))
 
         state = {"bank": 7, "done": 0, "loaded": 0, "copied": 0, "spare": 0}
-        raw, grp, codes, planes, nf_planes = {}, {}, {}, {}, {}
+        raw, grp, codes, planes, nf_planes, pools = {}, {}, {}, {}, {}, {}
+        pair_ring = []
         pending = []
         ring = []
 
         def raw_tile(u, shape, dtype):
             assert len(ring) < RAW_BUFS or ring[len(ring) - RAW_BUFS][0], "the oldest slot is still in use"
-            ring.append([False])
+            ring.append([0])
             raw[u] = (stage.tile(shape, dtype, name="raw", tag="raw", bufs=RAW_BUFS), ring[len(ring) - 1])
             return raw[u][0]
 
         def raw_done(u):
             t, flag = raw.pop(u)
-            flag[0] = True
+            flag[0] += 1
             return t
+
+        def may_load(u):
+            if u[0] == "inc" and u[1] == 0:
+                return len(pair_ring) < PAIR_BUFS or pair_ring[len(pair_ring) - PAIR_BUFS][0] == 2
+            if u[0] == "inc" and u[1] == 1:
+                return True
+            return slots_free(1 + state["spare"])
 
         def slots_free(n):
             return all([len(ring) + i < RAW_BUFS or ring[len(ring) + i - RAW_BUFS][0] for i in range(n)])
@@ -84,6 +93,15 @@ def tile_heterogeneoustemporalhypergraphnn_pa_l_kernel(tc, node_features, incide
             kind, a, b = u
             if kind == "nf":
                 src = node_features[a * K_PASS:(a + 1) * K_PASS, b * WIDE:(b + 1) * WIDE]
+            elif kind == "inc" and a < 2:
+                if a == 0:
+                    flag = [0]
+                    pair_ring.append(flag)
+                    t = pools["head"].tile([P, PACK, 2 * WIDE], BF16, name="pair", tag="pair", bufs=PAIR_BUFS)
+                    nc.sync.dma_start(out=t[:], in_=incidence[b * K_PASS:(b + 1) * K_PASS, 0:2 * WIDE].rearrange("(p j) w -> p j w", j=PACK))
+                    raw[("inc", 0, b)] = (t[:, :, 0:WIDE], flag)
+                    raw[("inc", 1, b)] = (t[:, :, WIDE:2 * WIDE], flag)
+                return
             elif kind == "inc":
                 src = incidence[b * K_PASS:(b + 1) * K_PASS, a * WIDE:(a + 1) * WIDE]
             else:
@@ -120,8 +138,8 @@ def tile_heterogeneoustemporalhypergraphnn_pa_l_kernel(tc, node_features, incide
                     c = keep.tile([P, WIDE], U32, name="ic%d" % b, tag="ic%d" % b, bufs=2, align_bytes=64)
                     s = keep.tile([P, WIDE], U8, name="is%d" % b, tag="is%d" % b, bufs=2, align_bytes=64)
                 elif kind == "w":
-                    c = keep.tile([P, WIDE], U32, name="wc%d_%d" % (a, b), tag="wc%d_%d" % (a, b), align_bytes=64)
-                    s = keep.tile([P, WIDE], U8, name="ws%d_%d" % (a, b), tag="ws%d_%d" % (a, b), align_bytes=64)
+                    c = pools["late"].tile([P, WIDE], U32, name="wc%d_%d" % (a, b), tag="wc%d_%d" % (a, b), align_bytes=64)
+                    s = pools["late"].tile([P, WIDE], U8, name="ws%d_%d" % (a, b), tag="ws%d_%d" % (a, b), align_bytes=64)
                 else:
                     c = keep.tile([P, WIDE], U32, name="ac%d" % b, tag="ac%d" % b, bufs=3, align_bytes=64)
                     s = keep.tile([P, WIDE], U8, name="as%d" % b, tag="as%d" % b, bufs=3, align_bytes=64)
@@ -134,7 +152,7 @@ def tile_heterogeneoustemporalhypergraphnn_pa_l_kernel(tc, node_features, incide
             while state["copied"] < min(k + 2, len(units)):
                 interleave(units[state["copied"]])
                 state["copied"] += 1
-            while state["loaded"] < len(units) and slots_free(1 + state["spare"]):
+            while state["loaded"] < len(units) and may_load(units[state["loaded"]]):
                 load(units[state["loaded"]])
                 state["loaded"] += 1
             quantize(units[k])
@@ -147,50 +165,6 @@ def tile_heterogeneoustemporalhypergraphnn_pa_l_kernel(tc, node_features, incide
         def pop(n):
             for i in range(min(n, len(pending))):
                 pending.pop(0)()
-
-        ident_b = keep.tile([P, P], BF16, name="ident_b", tag="ident_b")
-        ident_f = keep.tile([P, P], F32, name="ident_f", tag="ident_f")
-        a_rows = keep.tile([P, P], BF16, name="a_rows", tag="a_rows")
-        warm = keep.tile([P, 1], F32, name="warm", tag="warm")
-        ea_rows = edge_attention.rearrange("(c p) -> c p", p=P)
-        nc.scalar.dma_start(out=a_rows[0:16, :], in_=ea_rows[0:16, :])
-        nc.scalar.dma_start(out=a_rows[16:24, :], in_=ea_rows[16:24, :])
-        nc.scalar.dma_start(out=a_rows[24:32, :], in_=ea_rows[16:24, :])
-        nc.gpsimd.memset(a_rows[32:64, :], 0.0)
-        nc.gpsimd.memset(a_rows[64:128, :], 0.0)
-        nc.gpsimd.memset(warm[:], 0.0)
-        make_identity(nc, ident_b[:])
-        make_identity(nc, ident_f[:])
-        nc.scalar.activation(out=warm[:], in_=warm[:], func=ACT.Exp)
-        for i in range(RAW_BUFS):
-            load(units[i])
-        state["loaded"] = RAW_BUFS
-
-        a_col = keep.tile([P, N_TILES], F32, name="a_col", tag="a_col")
-        e_col = keep.tile([P, N_TILES], F32, name="e_col", tag="e_col")
-        attn = keep.tile([P, N_TILES], F32, name="attn", tag="attn")
-        stat = {}
-        for nm in ("pmax", "gmax", "nmax", "psumx", "gsum", "rsum"):
-            stat[nm] = keep.tile([P, 1], F32, name=nm, tag=nm)
-        a_t = new_bank([P, P], BF16)
-        nc.tensor.transpose(out=a_t[:], in_=a_rows[:], identity=ident_b[:])
-        nc.vector.tensor_copy(out=a_col[:], in_=a_t[:, 0:N_TILES])
-        nc.vector.reduce_max(out=stat["pmax"][:], in_=a_col[:], axis=AX.X)
-        state["bank"] = 7
-        m_t = new_bank([P, P], F32)
-        nc.tensor.matmul(out=m_t[:], lhsT=stat["pmax"][:].to_broadcast([P, P]), rhs=ident_f[:], start=True, stop=True)
-        nc.vector.reduce_max(out=stat["gmax"][:], in_=m_t[:], axis=AX.X)
-        nc.vector.tensor_scalar_mul(out=stat["nmax"][:], in0=stat["gmax"][:], scalar1=-1.0)
-        nc.scalar.activation(out=e_col[:], in_=a_col[:], func=ACT.Exp, bias=stat["nmax"][:], scale=1.0, accum_out=stat["psumx"][:])
-        state["bank"] = 7
-        s_t = new_bank([P, P], F32)
-        nc.tensor.matmul(out=s_t[:], lhsT=stat["psumx"][:].to_broadcast([P, P]), rhs=ident_f[:], start=True, stop=True)
-        interleave(units[0])
-        state["copied"] = 1
-        nc.vector.reduce_sum(out=stat["gsum"][:], in_=s_t[:], axis=AX.X)
-        nc.vector.reciprocal(out=stat["rsum"][:], in_=stat["gsum"][:])
-        nc.vector.tensor_scalar_mul(out=attn[:], in0=e_col[:], scalar1=stat["rsum"][:])
-        b1_all = keep.tile([P, N_CH], BF16, name="b1_all", tag="b1_all")
 
         def s1_step(chunks, g, q, banks):
             for j in chunks:
@@ -239,7 +213,7 @@ def tile_heterogeneoustemporalhypergraphnn_pa_l_kernel(tc, node_features, incide
             if k >= TAIL_GROUPS and k % 3 != 0:
                 ba = raw_tile(("ot", k), [P, WIDE], F32)
             else:
-                ba = stage.tile([P, WIDE], F32, name="ot", tag="ot", bufs=4)
+                ba = pools["late"].tile([P, WIDE], F32, name="ot", tag="ot", bufs=4)
             nc.scalar.activation(out=ba[:], in_=b1_all[:, n * WIDE:(n + 1) * WIDE], func=ACT.Copy, scale=attn[:, e_tile:e_tile + 1])
             bias_tiles[k] = ba
 
@@ -275,8 +249,7 @@ def tile_heterogeneoustemporalhypergraphnn_pa_l_kernel(tc, node_features, incide
                 nxt["mm"] += 1
                 pop(1)
 
-        base = 0
-        for g in range(NG):
+        def head_block(g, base):
             banks = {}
             for j in (0, 1):
                 for t in range(NT):
@@ -289,8 +262,59 @@ def tile_heterogeneoustemporalhypergraphnn_pa_l_kernel(tc, node_features, incide
                 s1_step((0, 1), g, q, banks)
                 if g == 1 and q == 0:
                     nc.sync.dma_start(out=b1_all[:], in_=b1.partition_broadcast(P))
-            base += HEAD_UNITS[g]
             empty_s1((0, 1), g, banks, E1_HEAD, False)
+
+        with tc.tile_pool(name="head", bufs=PAIR_BUFS) as head:
+            pools["head"] = head
+            ident_b = keep.tile([P, P], BF16, name="ident_b", tag="ident_b")
+            ident_f = keep.tile([P, P], F32, name="ident_f", tag="ident_f")
+            a_rows = keep.tile([P, P], BF16, name="a_rows", tag="a_rows")
+            warm = keep.tile([P, 1], F32, name="warm", tag="warm")
+            ea_rows = edge_attention.rearrange("(c p) -> c p", p=P)
+            nc.sync.dma_start(out=a_rows[0:16, :], in_=ea_rows[0:16, :])
+            nc.sync.dma_start(out=a_rows[16:24, :], in_=ea_rows[16:24, :])
+            nc.sync.dma_start(out=a_rows[24:32, :], in_=ea_rows[16:24, :])
+            nc.gpsimd.memset(a_rows[32:64, :], 0.0)
+            nc.gpsimd.memset(a_rows[64:128, :], 0.0)
+            nc.gpsimd.memset(warm[:], 0.0)
+            make_identity(nc, ident_b[:])
+            make_identity(nc, ident_f[:])
+            nc.scalar.activation(out=warm[:], in_=warm[:], func=ACT.Exp)
+            while may_load(units[state["loaded"]]):
+                load(units[state["loaded"]])
+                state["loaded"] += 1
+
+            a_col = keep.tile([P, N_TILES], F32, name="a_col", tag="a_col")
+            e_col = keep.tile([P, N_TILES], F32, name="e_col", tag="e_col")
+            attn = keep.tile([P, N_TILES], F32, name="attn", tag="attn")
+            stat = {}
+            for nm in ("pmax", "gmax", "nmax", "psumx", "gsum", "rsum"):
+                stat[nm] = keep.tile([P, 1], F32, name=nm, tag=nm)
+            a_t = new_bank([P, P], BF16)
+            nc.tensor.transpose(out=a_t[:], in_=a_rows[:], identity=ident_b[:])
+            nc.vector.tensor_copy(out=a_col[:], in_=a_t[:, 0:N_TILES])
+            nc.vector.reduce_max(out=stat["pmax"][:], in_=a_col[:], axis=AX.X)
+            state["bank"] = 7
+            m_t = new_bank([P, P], F32)
+            nc.tensor.matmul(out=m_t[:], lhsT=stat["pmax"][:].to_broadcast([P, P]), rhs=ident_f[:], start=True, stop=True)
+            nc.vector.reduce_max(out=stat["gmax"][:], in_=m_t[:], axis=AX.X)
+            nc.vector.tensor_scalar_mul(out=stat["nmax"][:], in0=stat["gmax"][:], scalar1=-1.0)
+            nc.scalar.activation(out=e_col[:], in_=a_col[:], func=ACT.Exp, bias=stat["nmax"][:], scale=1.0, accum_out=stat["psumx"][:])
+            state["bank"] = 7
+            s_t = new_bank([P, P], F32)
+            nc.tensor.matmul(out=s_t[:], lhsT=stat["psumx"][:].to_broadcast([P, P]), rhs=ident_f[:], start=True, stop=True)
+            interleave(units[0])
+            state["copied"] = 1
+            nc.vector.reduce_sum(out=stat["gsum"][:], in_=s_t[:], axis=AX.X)
+            nc.vector.reciprocal(out=stat["rsum"][:], in_=stat["gsum"][:])
+            nc.vector.tensor_scalar_mul(out=attn[:], in0=e_col[:], scalar1=stat["rsum"][:])
+            b1_all = keep.tile([P, N_CH], BF16, name="b1_all", tag="b1_all")
+
+            head_block(0, 0)
+        pools["late"] = ctx.enter_context(tc.tile_pool(name="late", bufs=1))
+        head_block(1, HEAD_UNITS[0])
+        head_block(2, HEAD_UNITS[0] + HEAD_UNITS[1])
+        base = sum(HEAD_UNITS)
 
         for j in range(2, NJ):
             for g in range(NG):

from contextlib import ExitStack

import concourse.mybir as mybir
from concourse.masks import make_identity

N_NODES, N_EDGES, N_CH = 6144, 3072, 1536
FLOPS = 2 * N_EDGES * N_NODES * N_CH + 2 * N_EDGES * N_CH * N_CH

F32 = mybir.dt.float32
BF16 = mybir.dt.bfloat16
U32 = mybir.dt.uint32
U8 = mybir.dt.uint8
FP8X4 = mybir.dt.float8_e4m3fn_x4
ACT = mybir.ActivationFunctionType
ALU = mybir.AluOpType
AX = mybir.AxisListType

P = 128
PACK = 4
K_PASS = P * PACK
WIDE = 512
NQ = N_NODES // K_PASS
NG = N_CH // K_PASS
NJ = N_EDGES // WIDE
NT = WIDE // P
N_TILES = N_EDGES // P

RAW_BUFS = 7
PAIR_BUFS = 4
GRP_BUFS = 3
V_COLS = 256
HEAD_UNITS = (38, 17, 16)
BLOCK_UNITS = {(2, 0): 7, (2, 1): 7, (2, 2): 7, (3, 0): 4, (3, 1): 4, (3, 2): 4, (4, 0): 4, (4, 1): 4, (4, 2): 5}
BATCH = {(2, 1): 6, (2, 2): 6, (3, 0): 6, (3, 1): 6, (3, 2): 6, (4, 0): 6, (4, 1): 6, (4, 2): 6, (5, 0): 4, (5, 1): 4, (5, 2): 4}
TAIL_GROUPS = 60
BA_AHEAD = 2
BA_AHEAD_TAIL = 5
E1_HEAD = "svssvssv"
E1_BODY = "svsv"


def tile_heterogeneoustemporalhypergraphnn_pa_l_kernel(tc, node_features, incidence, W1, b1, edge_attention, out):
    nc = tc.nc
    with ExitStack() as ctx:
        ctx.enter_context(tc.manual_schedule())
        keep = ctx.enter_context(tc.tile_pool(name="keep", bufs=1))
        stage = ctx.enter_context(tc.tile_pool(name="stage", bufs=2))
        psum = ctx.enter_context(tc.psum_pool(name="psum", bufs=1))

        state = {"bank": 7, "done": 0, "loaded": 0, "copied": 0, "spare": 0}
        raw, grp, codes, planes, nf_planes, pools = {}, {}, {}, {}, {}, {}
        pair_ring = []
        pending = []
        ring = []

        def raw_tile(u, shape, dtype):
            assert len(ring) < RAW_BUFS or ring[len(ring) - RAW_BUFS][0], "the oldest slot is still in use"
            ring.append([0])
            raw[u] = (stage.tile(shape, dtype, name="raw", tag="raw", bufs=RAW_BUFS), ring[len(ring) - 1])
            return raw[u][0]

        def raw_done(u):
            t, flag = raw.pop(u)
            flag[0] += 1
            return t

        def may_load(u):
            if u[0] == "inc" and u[1] == 0:
                return len(pair_ring) < PAIR_BUFS or pair_ring[len(pair_ring) - PAIR_BUFS][0] == 2
            if u[0] == "inc" and u[1] == 1:
                return True
            return slots_free(1 + state["spare"])

        def slots_free(n):
            return all([len(ring) + i < RAW_BUFS or ring[len(ring) + i - RAW_BUFS][0] for i in range(n)])

        def new_bank(shape, dtype):
            i = state["bank"]
            state["bank"] = (i + 1) % 8
            return psum.tile(shape, dtype, name="bank%d" % i, tag="bank%d" % i)

        units = []
        for q in range(NQ):
            units.extend([("nf", q, 0), ("inc", 0, q), ("inc", 1, q)])
        for g in (1, 2):
            units.extend([("nf", q, g) for q in range(NQ)])
        units.extend([("inc", 2, q) for q in range(NQ)])
        units.extend([("w", g, n) for g in range(NG) for n in range(NG)])
        for j in range(3, NJ):
            units.extend([("inc", j, q) for q in range(NQ)])

        def load(u):
            kind, a, b = u
            if kind == "nf":
                src = node_features[a * K_PASS:(a + 1) * K_PASS, b * WIDE:(b + 1) * WIDE]
            elif kind == "inc" and a < 2:
                if a == 0:
                    flag = [0]
                    pair_ring.append(flag)
                    t = pools["head"].tile([P, PACK, 2 * WIDE], BF16, name="pair", tag="pair", bufs=PAIR_BUFS)
                    nc.sync.dma_start(out=t[:], in_=incidence[b * K_PASS:(b + 1) * K_PASS, 0:2 * WIDE].rearrange("(p j) w -> p j w", j=PACK))
                    raw[("inc", 0, b)] = (t[:, :, 0:WIDE], flag)
                    raw[("inc", 1, b)] = (t[:, :, WIDE:2 * WIDE], flag)
                return
            elif kind == "inc":
                src = incidence[b * K_PASS:(b + 1) * K_PASS, a * WIDE:(a + 1) * WIDE]
            else:
                src = W1[a * K_PASS:(a + 1) * K_PASS, b * WIDE:(b + 1) * WIDE]
            t = raw_tile(u, [P, PACK, WIDE], BF16)
            nc.sync.dma_start(out=t[:], in_=src.rearrange("(p j) w -> p j w", j=PACK))

        def interleave(u):
            t = raw_done(u)
            o = stage.tile([P, PACK * WIDE], BF16, name="grp", tag="grp", bufs=GRP_BUFS, align_bytes=64)
            if u[0] == "nf":
                src = t[:].rearrange("p j (m t) -> p m j t", t=PACK)
                dst = o[:].rearrange("p (t m j) -> p m j t", t=PACK, j=PACK)
                nc.vector.tensor_copy(out=dst[:, 0:V_COLS // PACK], in_=src[:, 0:V_COLS // PACK])
                nc.scalar.copy(out=dst[:, V_COLS // PACK:P], in_=src[:, V_COLS // PACK:P])
            else:
                src = t[:].rearrange("p j (c i) -> p c j i", i=PACK)
                dst = o[:].rearrange("p (c i j) -> p c j i", i=PACK, j=PACK)
                nc.vector.tensor_copy(out=dst[:, 0:V_COLS // PACK], in_=src[:, 0:V_COLS // PACK])
                nc.scalar.copy(out=dst[:, V_COLS // PACK:P], in_=src[:, V_COLS // PACK:P])
            grp[u] = o

        def quantize(u):
            kind, a, b = u
            o = grp.pop(u)
            if kind == "nf":
                c = keep.tile([P, WIDE], U32, name="nfc%d_%d" % (a, b), tag="nfc%d_%d" % (a, b), align_bytes=64)
                if b == 0:
                    nf_planes[a] = keep.tile([P, WIDE], U8, name="nfs%d" % a, tag="nfs%d" % a, align_bytes=64)
                s = nf_planes[a][PACK * b:P, :]
                nc.vector.quantize_mx(out=c[:].bitcast(FP8X4), scales=s, in_=o[:])
            else:
                if kind == "inc":
                    c = keep.tile([P, WIDE], U32, name="ic%d" % b, tag="ic%d" % b, bufs=2, align_bytes=64)
                    s = keep.tile([P, WIDE], U8, name="is%d" % b, tag="is%d" % b, bufs=2, align_bytes=64)
                elif kind == "w":
                    c = pools["late"].tile([P, WIDE], U32, name="wc%d_%d" % (a, b), tag="wc%d_%d" % (a, b), align_bytes=64)
                    s = pools["late"].tile([P, WIDE], U8, name="ws%d_%d" % (a, b), tag="ws%d_%d" % (a, b), align_bytes=64)
                else:
                    c = keep.tile([P, WIDE], U32, name="ac%d" % b, tag="ac%d" % b, bufs=3, align_bytes=64)
                    s = keep.tile([P, WIDE], U8, name="as%d" % b, tag="as%d" % b, bufs=3, align_bytes=64)
                nc.vector.quantize_mx(out=c[:].bitcast(FP8X4), scales=s[:], in_=o[:])
            codes[u] = c
            planes[u] = s

        def pump():
            k = state["done"]
            while state["copied"] < min(k + 2, len(units)):
                interleave(units[state["copied"]])
                state["copied"] += 1
            while state["loaded"] < len(units) and may_load(units[state["loaded"]]):
                load(units[state["loaded"]])
                state["loaded"] += 1
            quantize(units[k])
            state["done"] = k + 1

        def advance(target):
            while state["done"] < min(target, len(units)):
                pump()

        def pop(n):
            for i in range(min(n, len(pending))):
                pending.pop(0)()

        def s1_step(chunks, g, q, banks):
            for j in chunks:
                for t in range(NT):
                    nc.tensor.matmul_mx(out=banks[(j, t)][:],
                                        lhsT=codes[("nf", q, g)][:, t * P:(t + 1) * P].bitcast(FP8X4),
                                        lhsT_scale=planes[("nf", q, g)][:, t * P:(t + 1) * P],
                                        rhs=codes[("inc", j, q)][:].bitcast(FP8X4),
                                        rhs_scale=planes[("inc", j, q)][:],
                                        start=(q == 0), stop=(q == NQ - 1))

        def empty_s1(chunks, g, banks, who, split):
            i = 0
            for j in chunks:
                ab = raw_tile(("agg", j, g), [P, PACK, WIDE], BF16)
                for t in range(NT):
                    if who[i] == "s":
                        nc.scalar.copy(out=ab[:, t, :], in_=banks[(j, t)][:])
                    else:
                        nc.vector.tensor_copy(out=ab[:, t, :], in_=banks[(j, t)][:])
                    i += 1
            for j in chunks:
                pending.append(lambda j=j: agg_interleave(("agg", j, g), split))
                pending.append(lambda j=j: quantize(("agg", j, g)))

        def agg_interleave(u, split):
            ab = raw_done(u)
            o = stage.tile([P, PACK * WIDE], BF16, name="grp", tag="grp", bufs=GRP_BUFS, align_bytes=64)
            src = ab[:].rearrange("p t (c i) -> p c t i", i=PACK)
            dst = o[:].rearrange("p (c i t) -> p c t i", i=PACK, t=PACK)
            if split:
                nc.vector.tensor_copy(out=dst[:, 0:V_COLS // PACK], in_=src[:, 0:V_COLS // PACK])
                nc.scalar.copy(out=dst[:, V_COLS // PACK:P], in_=src[:, V_COLS // PACK:P])
            else:
                nc.vector.tensor_copy(out=dst, in_=src)
            grp[u] = o

        groups = [(j, m, n) for j in range(NJ) for m in range(NT) for n in range(NG)]
        bias_tiles = {}
        s2_banks = {}
        nxt = {"mm": 0, "ba": 0}

        def bias_tile(k):
            j, m, n = groups[k]
            e_tile = j * NT + m
            if k >= TAIL_GROUPS and k % 3 != 0:
                ba = raw_tile(("ot", k), [P, WIDE], F32)
            else:
                ba = pools["late"].tile([P, WIDE], F32, name="ot", tag="ot", bufs=4)
            nc.scalar.activation(out=ba[:], in_=b1_all[:, n * WIDE:(n + 1) * WIDE], func=ACT.Copy, scale=attn[:, e_tile:e_tile + 1])
            bias_tiles[k] = ba

        def s2_group(k):
            j, m, n = groups[k]
            bank = new_bank([P, WIDE], F32)
            for g in range(NG):
                nc.tensor.matmul_mx(out=bank[:],
                                    lhsT=codes[("agg", j, g)][:, m * P:(m + 1) * P].bitcast(FP8X4),
                                    lhsT_scale=planes[("agg", j, g)][:, m * P:(m + 1) * P],
                                    rhs=codes[("w", g, n)][:].bitcast(FP8X4),
                                    rhs_scale=planes[("w", g, n)][:],
                                    start=(g == 0), stop=(g == NG - 1))
            s2_banks[k] = bank
            pending.append(lambda: finish(k))

        def finish(k):
            j, m, n = groups[k]
            e_tile = j * NT + m
            ot = bias_tiles.pop(k)
            nc.vector.scalar_tensor_tensor(out=ot[:], in0=s2_banks.pop(k)[:], scalar=attn[:, e_tile:e_tile + 1],
                                           in1=ot[:], op0=ALU.mult, op1=ALU.add)
            nc.sync.dma_start(out=out[e_tile * P:(e_tile + 1) * P, n * WIDE:(n + 1) * WIDE], in_=ot[:])
            if ("ot", k) in raw:
                raw_done(("ot", k))
            while nxt["ba"] < min(k + 1 + (BA_AHEAD_TAIL if k + 1 >= TAIL_GROUPS else BA_AHEAD), len(groups)):
                bias_tile(nxt["ba"])
                nxt["ba"] += 1

        def batch(n):
            for i in range(n):
                s2_group(nxt["mm"])
                nxt["mm"] += 1
                pop(1)

        def head_block(g, base):
            banks = {}
            for j in (0, 1):
                for t in range(NT):
                    banks[(j, t)] = new_bank([P, WIDE], F32)
            for q in range(NQ):
                if q == NQ - 3:
                    state["spare"] = 2
                advance(base + (HEAD_UNITS[g] * (q + 1) + NQ - 1) // NQ)
                pop(1)
                s1_step((0, 1), g, q, banks)
                if g == 1 and q == 0:
                    nc.sync.dma_start(out=b1_all[:], in_=b1.partition_broadcast(P))
            empty_s1((0, 1), g, banks, E1_HEAD, False)

        with tc.tile_pool(name="head", bufs=PAIR_BUFS) as head:
            pools["head"] = head
            ident_b = keep.tile([P, P], BF16, name="ident_b", tag="ident_b")
            ident_f = keep.tile([P, P], F32, name="ident_f", tag="ident_f")
            a_rows = keep.tile([P, P], BF16, name="a_rows", tag="a_rows")
            warm = keep.tile([P, 1], F32, name="warm", tag="warm")
            ea_rows = edge_attention.rearrange("(c p) -> c p", p=P)
            nc.sync.dma_start(out=a_rows[0:16, :], in_=ea_rows[0:16, :])
            nc.sync.dma_start(out=a_rows[16:24, :], in_=ea_rows[16:24, :])
            nc.sync.dma_start(out=a_rows[24:32, :], in_=ea_rows[16:24, :])
            nc.gpsimd.memset(a_rows[32:64, :], 0.0)
            nc.gpsimd.memset(a_rows[64:128, :], 0.0)
            nc.gpsimd.memset(warm[:], 0.0)
            make_identity(nc, ident_b[:])
            make_identity(nc, ident_f[:])
            nc.scalar.activation(out=warm[:], in_=warm[:], func=ACT.Exp)
            while may_load(units[state["loaded"]]):
                load(units[state["loaded"]])
                state["loaded"] += 1

            a_col = keep.tile([P, N_TILES], F32, name="a_col", tag="a_col")
            e_col = keep.tile([P, N_TILES], F32, name="e_col", tag="e_col")
            attn = keep.tile([P, N_TILES], F32, name="attn", tag="attn")
            stat = {}
            for nm in ("pmax", "gmax", "nmax", "psumx", "gsum", "rsum"):
                stat[nm] = keep.tile([P, 1], F32, name=nm, tag=nm)
            a_t = new_bank([P, P], BF16)
            nc.tensor.transpose(out=a_t[:], in_=a_rows[:], identity=ident_b[:])
            nc.vector.tensor_copy(out=a_col[:], in_=a_t[:, 0:N_TILES])
            nc.vector.reduce_max(out=stat["pmax"][:], in_=a_col[:], axis=AX.X)
            state["bank"] = 7
            m_t = new_bank([P, P], F32)
            nc.tensor.matmul(out=m_t[:], lhsT=stat["pmax"][:].to_broadcast([P, P]), rhs=ident_f[:], start=True, stop=True)
            nc.vector.reduce_max(out=stat["gmax"][:], in_=m_t[:], axis=AX.X)
            nc.vector.tensor_scalar_mul(out=stat["nmax"][:], in0=stat["gmax"][:], scalar1=-1.0)
            nc.scalar.activation(out=e_col[:], in_=a_col[:], func=ACT.Exp, bias=stat["nmax"][:], scale=1.0, accum_out=stat["psumx"][:])
            state["bank"] = 7
            s_t = new_bank([P, P], F32)
            nc.tensor.matmul(out=s_t[:], lhsT=stat["psumx"][:].to_broadcast([P, P]), rhs=ident_f[:], start=True, stop=True)
            interleave(units[0])
            state["copied"] = 1
            nc.vector.reduce_sum(out=stat["gsum"][:], in_=s_t[:], axis=AX.X)
            nc.vector.reciprocal(out=stat["rsum"][:], in_=stat["gsum"][:])
            nc.vector.tensor_scalar_mul(out=attn[:], in0=e_col[:], scalar1=stat["rsum"][:])
            b1_all = keep.tile([P, N_CH], BF16, name="b1_all", tag="b1_all")

            head_block(0, 0)
        pools["late"] = ctx.enter_context(tc.tile_pool(name="late", bufs=1))
        head_block(1, HEAD_UNITS[0])
        head_block(2, HEAD_UNITS[0] + HEAD_UNITS[1])
        base = sum(HEAD_UNITS)

        for j in range(2, NJ):
            for g in range(NG):
                banks = {}
                for t in range(NT):
                    banks[(j, t)] = new_bank([P, WIDE], F32)
                n_units = BLOCK_UNITS.get((j, g), 0)
                state["spare"] = 1
                for q in range(NQ):
                    advance(base + (n_units * (q + 1) + NQ - 1) // NQ)
                    pop(1)
                    s1_step((j,), g, q, banks)
                base += n_units
                last = (j == NJ - 1 and g == NG - 1)
                empty_s1((j,), g, banks, E1_BODY, last)
                if (j, g) == (2, 1):
                    for i in range(BA_AHEAD):
                        bias_tile(i)
                    nxt["ba"] = BA_AHEAD
                batch(BATCH.get((j, g), 0))
        pop(len(pending))
        while nxt["mm"] < len(groups):
            s2_group(nxt["mm"])
            nxt["mm"] += 1
            pop(1)
        pop(len(pending))
